import numpy as np
import ml_dtypes


def mxq(x, axis, fmt="e4m3"):
    dtype, down = {"e4m3": (ml_dtypes.float8_e4m3fn, 7), "e5m2": (ml_dtypes.float8_e5m2, 14)}[fmt]
    v = np.moveaxis(np.asarray(x, np.float32).astype(ml_dtypes.bfloat16).astype(np.float64), axis, -1)
    blocks = v.reshape(v.shape[:-1] + (-1, 32))
    amax = np.abs(blocks).max(-1, keepdims=True)
    byte = np.maximum(np.where(amax > 0, np.frexp(amax)[1] - 1 + 127, 0) - down, 1)
    scale = np.exp2(byte - 127.0)
    codes = (blocks / scale).astype(np.float32).astype(dtype).astype(np.float64)
    return np.moveaxis((codes * scale).reshape(v.shape), -1, axis)


WIDE = False


def mx_kscale(k):
    if not WIDE:
        return np.ones(k)
    levels = np.array([10, -10, 5, -5, 0])
    if k % 512:
        return np.exp2(np.random.permutation(np.resize(levels, k // 32))).repeat(32)
    a = np.empty((k // 512, 16))
    for p in range(k // 512):
        a[p, :8] = np.random.permutation(np.resize(levels, 8))
        for g in range(8):
            far = levels[np.abs(levels - a[p, g]) >= 10]
            a[p, g + 8] = far[np.random.randint(len(far))]
    return np.exp2(a.ravel()).repeat(32)


BF16 = ml_dtypes.bfloat16


def bf(x):
    return np.asarray(x, np.float32).astype(BF16)


def f64(x):
    return np.asarray(x).astype(np.float64)


B, IN, H, OUT, L, STEPS = 1024, 512, 1024, 128, 3, 3
LN_EPS = 1e-5
TAU_EPS = 1e-6


def layer_norm(v, g, b):
    m = v.mean(-1, keepdims=True)
    var = ((v - m) ** 2).mean(-1, keepdims=True)
    return (v - m) / np.sqrt(var + LN_EPS) * g + b


def setup_inputs():
    r = mx_kscale(IN)
    s = mx_kscale(H)
    s = s / s.max()
    t = mx_kscale(H)
    liq_rms = np.sqrt(L * (L + 1) / 2.0)
    return {"liq": bf(np.random.standard_normal((B, H)) * liq_rms * s),
            "h": bf(np.random.standard_normal((B, H))),
            "x": bf(np.random.standard_normal((B, IN)) * r),
            "W_in": bf(np.random.standard_normal((H, IN)) * 0.7 / np.sqrt(IN) / r),
            "b_in": bf(np.random.standard_normal(H) * 0.3),
            "W_v": bf(np.random.standard_normal((H, H)) / np.sqrt(H) * t[:, None] / s),
            "b_v": bf(np.random.standard_normal(H) * 0.5 * t),
            "W_o": bf(np.random.standard_normal((H, H)) / np.sqrt(H) / t),
            "b_o": bf(np.random.standard_normal(H) * 0.5),
            "g_att": bf(1.0 + 0.1 * np.random.standard_normal(H)),
            "beta_att": bf(np.random.standard_normal(H) * 0.3),
            "tau": bf(0.5 + 0.5 * np.random.random(H))}


def reference(liq, h, x, W_in, b_in, W_v, b_v, W_o, b_o, g_att, beta_att, tau):
    liq, h = f64(liq), f64(h)
    xin = (mxq(f64(x), 1, "e4m3") @ mxq(f64(W_in), 1, "e4m3").T) + f64(b_in)
    v = (mxq(liq, 1, "e4m3") @ mxq(f64(W_v), 1, "e4m3").T) + f64(b_v)
    att = (mxq(v, 1, "e4m3") @ mxq(f64(W_o), 1, "e4m3").T) + f64(b_o)
    z = layer_norm(att + liq, f64(g_att), f64(beta_att))
    dh = (-h + np.tanh(z + xin)) / (f64(tau) + TAU_EPS)
    return h + dh

@@ -1,0 +1,313 @@
+from contextlib import ExitStack
+
+import concourse.mybir as mybir
+from concourse.masks import make_identity
+
+F32 = mybir.dt.float32
+BF16 = mybir.dt.bfloat16
+U32 = mybir.dt.uint32
+U8 = mybir.dt.uint8
+FP8X4 = mybir.dt.float8_e4m3fn_x4
+ALU = mybir.AluOpType
+ACT = mybir.ActivationFunctionType
+
+P = 128
+B, IN, H = 1024, 512, 1024
+K_PASS = 512
+BANK = 512
+CHUNK = 512
+TILES = CHUNK // P
+LN_EPS = 1e-5
+TAU_EPS = 1e-6
+SQRT_H = 32.0
+
+FLOPS = 2 * B * H * (IN + H + H)
+
+
+def tile_advancedliquidneuralnetwork_pb_kernel(
+    tc, liq, h, x, W_in, b_in, W_v, b_v, W_o, b_o, g_att, beta_att, tau, out
+):
+    nc = tc.nc
+    with ExitStack() as ctx:
+        consts = ctx.enter_context(tc.tile_pool(name="consts", bufs=1))
+        keep = ctx.enter_context(tc.tile_pool(name="keep", bufs=1))
+        raw = ctx.enter_context(tc.tile_pool(name="raw", bufs=4))
+        stage = ctx.enter_context(tc.tile_pool(name="stage", bufs=2))
+        work = ctx.enter_context(tc.tile_pool(name="work", bufs=3))
+        small = ctx.enter_context(tc.tile_pool(name="small", bufs=4))
+        psum = ctx.enter_context(tc.psum_pool(name="psum", bufs=8))
+
+        ident = consts.tile([P, P], F32)
+        make_identity(nc, ident[:])
+        ones = consts.tile([P, P], BF16)
+        nc.vector.memset(ones[:], 1.0)
+        minus_half = consts.tile([P, 1], F32)
+        nc.vector.memset(minus_half[:], -0.5)
+
+        bv = consts.tile([P, 8], BF16)
+        nc.scalar.dma_start(
+            out=bv[:].rearrange("p (g t) -> p g t", t=4),
+            in_=b_v.rearrange("(g p t) -> p g t", p=P, t=4),
+        )
+
+        vec_rows = stage.tile([P, 3, H], BF16, tag="staged", align_bytes=64)
+        nc.vector.memset(vec_rows[:], 0.0)
+        for n, vector in enumerate((b_o, g_att, tau)):
+            nc.scalar.dma_start(
+                out=vec_rows[0:1, n, :], in_=vector.rearrange("(o n) -> o n", o=1)
+            )
+
+        warm = consts.tile([P, 2], F32)
+        nc.vector.memset(warm[:], 0.0)
+        nc.scalar.activation(out=warm[:, 1:2], in_=warm[:, 0:1], func=ACT.Tanh)
+
+        liq_rows = liq.rearrange("(q p i) k -> q p i k", q=2, i=TILES)
+        h_rows = h.rearrange("(q p i) k -> q p i k", q=2, i=TILES)
+        out_rows = out.rearrange("(q p i) n -> q p i n", q=2, i=TILES)
+        wv_rows = W_v.rearrange("(g p t) k -> g p t k", g=2, t=4)
+        wo_rows = W_o.rearrange("(q j p) k -> q p j k", q=2, p=P)
+
+        liq_raw = [keep.tile([P, TILES, H], BF16, name="liq_raw%d" % q) for q in range(2)]
+        wv_raw = [raw.tile([P, TILES, H], BF16, name="wv_raw%d" % g, tag="raw") for g in range(2)]
+        wo_raw = [raw.tile([P, TILES, H], BF16, name="wo_raw%d" % q, tag="raw") for q in range(2)]
+        for q in range(2):
+            nc.sync.dma_start(out=liq_raw[q][:], in_=liq_rows[q])
+        for g in range(2):
+            nc.sync.dma_start(out=wv_raw[g][:], in_=wv_rows[g])
+        for q in range(2):
+            nc.sync.dma_start(out=wo_raw[q][:], in_=wo_rows[q])
+
+        bo_all = consts.tile([P, H], BF16)
+        g_all = consts.tile([P, H], BF16)
+        r_all = consts.tile([P, H], F32)
+        one_minus_r = consts.tile([P, H], F32)
+
+        def spread_vectors():
+            for half in range(2):
+                cols = slice(half * BANK, (half + 1) * BANK)
+                spread = [
+                    psum.tile([P, BANK], F32, name="spread%d" % n, tag="bank") for n in range(3)
+                ]
+                for n in range(3):
+                    nc.tensor.matmul(
+                        spread[n][:], lhsT=ones[:], rhs=vec_rows[:, n, cols], start=True, stop=True
+                    )
+                nc.scalar.copy(out=bo_all[:, cols], in_=spread[0][:])
+                nc.scalar.mul(out=g_all[:, cols], in_=spread[1][:], mul=SQRT_H)
+                nc.vector.tensor_scalar_add(out=r_all[:, cols], in0=spread[2][:], scalar1=TAU_EPS)
+            nc.vector.reciprocal(out=r_all[:], in_=r_all[:])
+            nc.gpsimd.tensor_scalar(
+                out=one_minus_r[:], in0=r_all[:], scalar1=-1.0, scalar2=1.0,
+                op0=ALU.mult, op1=ALU.add,
+            )
+
+        def mx_operand(name, passes):
+            codes = keep.tile([P, passes, 1024], U32, name=name + "_codes", align_bytes=64)
+            scales = keep.tile([P, passes, 1024], U8, name=name + "_scales", align_bytes=64)
+            return codes, scales
+
+        liq_mx = mx_operand("liq", 2)
+        wv_mx = mx_operand("wv", 2)
+        v_mx = mx_operand("v", 2)
+        wo_mx = mx_operand("wo", 2)
+        x_mx = mx_operand("x", 1)
+        win_mx = mx_operand("win", 1)
+
+        def transpose_four(word_blocks, grouped_words):
+            bank = psum.tile([P, 4, P], F32, tag="bank")
+            for n, block in enumerate(word_blocks):
+                nc.tensor.transpose(bank[:, n, :], block, ident[:])
+            nc.scalar.copy(out=grouped_words, in_=bank[:].rearrange("p (a u) r -> p a r u", u=2))
+
+        def quantise(grouped, c, operand, cols):
+            codes, scales = operand
+            nc.vector.quantize_mx(
+                out=codes[:, c, cols].bitcast(FP8X4),
+                scales=scales[:, c, cols],
+                in_=grouped[:, c, :, :].rearrange("p r t -> p (r t)"),
+            )
+
+        def prepare_k1024(rows_raw, operand, chunk):
+            words = rows_raw[:].bitcast(F32)
+            grouped = stage.tile([P, 2, CHUNK, 4], BF16, tag="staged", align_bytes=64)
+            grouped_words = grouped[:].bitcast(F32)
+            for i in range(TILES):
+                transpose_four(
+                    [words[:, i, 256 * a + u : 256 * (a + 1) : 2] for a in range(2) for u in range(2)],
+                    grouped_words[:, :, i * P : (i + 1) * P, :],
+                )
+            for c in range(2):
+                quantise(grouped, c, operand, slice(chunk * CHUNK, (chunk + 1) * CHUNK))
+
+        def prepare_k512(rows_raw, operand):
+            words = rows_raw[:].bitcast(F32)
+            grouped = stage.tile([P, 1, 1024, 4], BF16, tag="staged", align_bytes=64)
+            grouped_words = grouped[:].bitcast(F32)
+            for j in range(0, 8, 2):
+                transpose_four(
+                    [words[:, j + a, u:256:2] for a in range(2) for u in range(2)],
+                    grouped_words[:, 0, j * P : (j + 2) * P, :].rearrange(
+                        "p (a r) u -> p a r u", a=2
+                    ),
+                )
+            quantise(grouped, 0, operand, slice(0, 1024))
+
+        def mx_matmul(acc, stationary, s_cols, moving, m_cols, passes):
+            for c in range(passes):
+                nc.tensor.matmul_mx(
+                    out=acc,
+                    lhsT=stationary[0][:, c, s_cols].bitcast(FP8X4),
+                    lhsT_scale=stationary[1][:, c, s_cols],
+                    rhs=moving[0][:, c, m_cols].bitcast(FP8X4),
+                    rhs_scale=moving[1][:, c, m_cols],
+                    start=(c == 0),
+                    stop=(c == passes - 1),
+                )
+
+        def tile_cols(n):
+            return slice(n * P, (n + 1) * P)
+
+        def compute_v(n):
+            grouped = stage.tile([P, 2, P, 4], BF16, tag="v_grouped", bufs=3, align_bytes=64)
+            for g in range(2):
+                bank = psum.tile([P, 4, P], F32, tag="bank")
+                for t in range(4):
+                    mx_matmul(bank[:, t, :], wv_mx, tile_cols(4 * g + t), liq_mx, tile_cols(n), 2)
+                nc.vector.tensor_tensor(
+                    out=grouped[:, g, :, :],
+                    in0=bank[:].rearrange("p t r -> p r t"),
+                    in1=bv[:, 4 * g : 4 * g + 4].unsqueeze(1).to_broadcast([P, P, 4]),
+                    op=ALU.add,
+                )
+            for g in range(2):
+                quantise(grouped, g, v_mx, tile_cols(n))
+
+        xin_t = keep.tile([P, 8, B], F32)
+        xin_bias = consts.tile([P, 8], F32)
+
+        def compute_xin(q, features):
+            cols = slice(q * CHUNK, (q + 1) * CHUNK)
+            for j in features:
+                bank = psum.tile([P, BANK], F32, tag="bank")
+                mx_matmul(bank[:], win_mx, tile_cols(j), x_mx, cols, 1)
+                nc.scalar.activation(
+                    out=xin_t[:, j, cols], in_=bank[:], func=ACT.Identity,
+                    bias=xin_bias[:, j : j + 1], scale=1.0,
+                )
+
+        residual, u_of, y_of, minus_mean_of, rstd_of, kept_of = {}, {}, {}, {}, {}, {}
+        bank_cols = [slice(k * BANK, (k + 1) * BANK) for k in range(2)]
+
+        def add_bias_to_liq(n):
+            q, i = divmod(n, TILES)
+            residual[n] = work.tile([P, H], F32, name="residual", tag="residual", bufs=8)
+            nc.gpsimd.tensor_tensor(
+                out=residual[n][:], in0=liq_raw[q][:, i, :], in1=bo_all[:], op=ALU.add
+            )
+
+        def statistics(n):
+            u = work.tile([P, H], F32, tag="u", bufs=2)
+            y = work.tile([P, H], F32, tag="y", bufs=4)
+            sums = small.tile([P, 2], F32, tag="sums")
+            for k, cols in enumerate(bank_cols):
+                att = psum.tile([P, BANK], F32, tag="bank")
+                mx_matmul(att[:], v_mx, tile_cols(n), wo_mx, cols, 2)
+                nc.vector.scalar_tensor_tensor(
+                    out=u[:, cols], in0=att[:], scalar=1.0, in1=residual[n][:, cols],
+                    op0=ALU.mult, op1=ALU.add, accum_out=sums[:, k : k + 1],
+                )
+            minus_mean = small.tile([P, 1], F32, tag="minus_mean")
+            nc.vector.tensor_scalar(
+                out=minus_mean[:], in0=sums[:, 0:1], scalar1=sums[:, 1:2], scalar2=-1.0 / H,
+                op0=ALU.add, op1=ALU.mult,
+            )
+            square_sum = small.tile([P, 1], F32, tag="square_sum")
+            nc.scalar.activation(
+                out=y[:], in_=u[:], func=ACT.Square, bias=minus_mean[:], scale=1.0,
+                accum_out=square_sum[:],
+            )
+            rstd = small.tile([P, 1], F32, tag="rstd")
+            nc.gpsimd.tensor_scalar_add(out=rstd[:], in0=square_sum[:], scalar1=H * LN_EPS)
+            nc.gpsimd.tensor_tensor(out=rstd[:], in0=rstd[:], in1=minus_half[:], op=ALU.pow)
+            u_of[n], y_of[n], minus_mean_of[n], rstd_of[n] = u, y, minus_mean, rstd
+
+        def centre_and_scale(n):
+            q, i = divmod(n, TILES)
+            kept_of[n] = work.tile([P, H], F32, name="kept", tag="kept", bufs=2)
+            nc.gpsimd.tensor_tensor(
+                out=kept_of[n][:], in0=h_raw[q][:, i, :], in1=one_minus_r[:], op=ALU.mult
+            )
+            nc.vector.scalar_tensor_tensor(
+                out=y_of[n][:], in0=u_of[n][:], scalar=minus_mean_of[n][:], in1=g_all[:],
+                op0=ALU.add, op1=ALU.mult,
+            )
+
+        def add_xin_and_tanh(n):
+            y = y_of[n]
+            xin = [psum.tile([P, 4, P], F32, name="xin%d" % k, tag="bank") for k in range(2)]
+            for j in range(8):
+                nc.tensor.transpose(xin[j // 4][:, j % 4, :], xin_t[:, j, tile_cols(n)], ident[:])
+            for k, cols in enumerate(bank_cols):
+                nc.vector.scalar_tensor_tensor(
+                    out=y[:, cols], in0=y[:, cols], scalar=rstd_of[n][:],
+                    in1=xin[k][:].rearrange("p a r -> p (a r)"), op0=ALU.mult, op1=ALU.add,
+                )
+            nc.scalar.activation(out=y[:], in_=y[:], func=ACT.Tanh)
+
+        def times_r(n):
+            nc.vector.tensor_tensor(out=y_of[n][:], in0=y_of[n][:], in1=r_all[:], op=ALU.mult)
+
+        def add_kept_and_store(n):
+            q, i = divmod(n, TILES)
+            y = y_of[n]
+            nc.vector.tensor_tensor(out=y[:], in0=y[:], in1=kept_of[n][:], op=ALU.add)
+            nc.sync.dma_start(out=out_rows[q][:, i, :], in_=y[:])
+
+        prepare_k1024(liq_raw[0], liq_mx, 0)
+        spread_vectors()
+        prepare_k1024(liq_raw[1], liq_mx, 1)
+        for n in range(8):
+            add_bias_to_liq(n)
+        for g in range(2):
+            prepare_k1024(wv_raw[g], wv_mx, g)
+
+        win_raw = raw.tile([P, 8, IN], BF16, tag="raw")
+        x_raw = raw.tile([P, 8, IN], BF16, tag="raw")
+        nc.sync.dma_start(out=win_raw[:], in_=W_in.rearrange("(j p) k -> p j k", p=P))
+        nc.sync.dma_start(
+            out=x_raw[:].rearrange("p (q i) k -> p q i k", q=2),
+            in_=x.rearrange("(q p i) k -> p q i k", q=2, i=TILES),
+        )
+        beta_t = consts.tile([P, 8], BF16)
+        bin_t = consts.tile([P, 8], BF16)
+        with nc.allow_non_contiguous_dma(reason="two vectors of 1024, one element a partition"):
+            nc.sync.dma_start(out=beta_t[:], in_=beta_att.rearrange("(j p) -> p j", p=P))
+            nc.sync.dma_start(out=bin_t[:], in_=b_in.rearrange("(j p) -> p j", p=P))
+
+        prepare_k1024(wo_raw[0], wo_mx, 0)
+        compute_v(0)
+        compute_v(1)
+        prepare_k1024(wo_raw[1], wo_mx, 1)
+        h_raw = [raw.tile([P, TILES, H], BF16, name="h_raw%d" % q, tag="raw") for q in range(2)]
+        for q in range(2):
+            nc.sync.dma_start(out=h_raw[q][:], in_=h_rows[q])
+        compute_v(2)
+        compute_v(3)
+        prepare_k512(win_raw, win_mx)
+        prepare_k512(x_raw, x_mx)
+        nc.vector.tensor_tensor(out=xin_bias[:], in0=beta_t[:], in1=bin_t[:], op=ALU.add)
+
+        for n in range(8 + 2):
+            if n < 8:
+                statistics(n)
+            if n < TILES:
+                compute_xin(n // 2, range(4 * (n % 2), 4 * (n % 2) + 4))
+                compute_v(n + TILES)
+            if 0 <= n - 1 < 8:
+                centre_and_scale(n - 1)
+            if 0 <= n - 2 < 8:
+                times_r(n - 2)
+            if 0 <= n - 1 < 8:
+                add_xin_and_tanh(n - 1)
+            if 0 <= n - 2 < 8:
+                add_kept_and_store(n - 2)

@@ -17,6 +17,8 @@ K_PASS = 512
 BANK = 512
 CHUNK = 512
 TILES = CHUNK // P
+GROUP = 2
+GCOLS = GROUP * P
 LN_EPS = 1e-5
 TAU_EPS = 1e-6
 SQRT_H = 32.0
@@ -33,33 +35,9 @@ def tile_advancedliquidneuralnetwork_pb_kernel(
         keep = ctx.enter_context(tc.tile_pool(name="keep", bufs=1))
         raw = ctx.enter_context(tc.tile_pool(name="raw", bufs=4))
         stage = ctx.enter_context(tc.tile_pool(name="stage", bufs=2))
-        work = ctx.enter_context(tc.tile_pool(name="work", bufs=3))
+        work = ctx.enter_context(tc.tile_pool(name="work", bufs=2))
         small = ctx.enter_context(tc.tile_pool(name="small", bufs=4))
         psum = ctx.enter_context(tc.psum_pool(name="psum", bufs=8))
-
-        ident = consts.tile([P, P], F32)
-        make_identity(nc, ident[:])
-        ones = consts.tile([P, P], BF16)
-        nc.vector.memset(ones[:], 1.0)
-        minus_half = consts.tile([P, 1], F32)
-        nc.vector.memset(minus_half[:], -0.5)
-
-        bv = consts.tile([P, 8], BF16)
-        nc.scalar.dma_start(
-            out=bv[:].rearrange("p (g t) -> p g t", t=4),
-            in_=b_v.rearrange("(g p t) -> p g t", p=P, t=4),
-        )
-
-        vec_rows = stage.tile([P, 3, H], BF16, tag="staged", align_bytes=64)
-        nc.vector.memset(vec_rows[:], 0.0)
-        for n, vector in enumerate((b_o, g_att, tau)):
-            nc.scalar.dma_start(
-                out=vec_rows[0:1, n, :], in_=vector.rearrange("(o n) -> o n", o=1)
-            )
-
-        warm = consts.tile([P, 2], F32)
-        nc.vector.memset(warm[:], 0.0)
-        nc.scalar.activation(out=warm[:, 1:2], in_=warm[:, 0:1], func=ACT.Tanh)
 
         liq_rows = liq.rearrange("(q p i) k -> q p i k", q=2, i=TILES)
         h_rows = h.rearrange("(q p i) k -> q p i k", q=2, i=TILES)
@@ -67,39 +45,74 @@ def tile_advancedliquidneuralnetwork_pb_kernel(
         wv_rows = W_v.rearrange("(g p t) k -> g p t k", g=2, t=4)
         wo_rows = W_o.rearrange("(q j p) k -> q p j k", q=2, p=P)
 
+        vec_rows = consts.tile([P, P], BF16)
+        nc.vector.memset(vec_rows[:], 0.0)
+        ident = consts.tile([P, P], F32)
+        make_identity(nc, ident[:])
+        ident_bf = consts.tile([P, P], BF16)
+        nc.vector.tensor_copy(out=ident_bf[:], in_=ident[:])
+        minus_half = consts.tile([P, 1], F32)
+        nc.vector.memset(minus_half[:], -0.5)
+
         liq_raw = [keep.tile([P, TILES, H], BF16, name="liq_raw%d" % q) for q in range(2)]
         wv_raw = [raw.tile([P, TILES, H], BF16, name="wv_raw%d" % g, tag="raw") for g in range(2)]
         wo_raw = [raw.tile([P, TILES, H], BF16, name="wo_raw%d" % q, tag="raw") for q in range(2)]
-        for q in range(2):
-            nc.sync.dma_start(out=liq_raw[q][:], in_=liq_rows[q])
+        for n, vector in enumerate((b_o, g_att, tau, beta_att, b_in)):
+            nc.sync.dma_start(
+                out=vec_rows[8 * n : 8 * n + 8, :], in_=vector.rearrange("(j p) -> j p", p=P)
+            )
+        bv = consts.tile([P, 8], BF16)
+        nc.sync.dma_start(
+            out=bv[:].rearrange("p (g t) -> p g t", t=4),
+            in_=b_v.rearrange("(g p t) -> p g t", p=P, t=4),
+        )
+
+        for i in range(0, TILES, 2):
+            nc.sync.dma_start(out=liq_raw[0][:, i : i + 2, :], in_=liq_rows[0][:, i : i + 2, :])
         for g in range(2):
             nc.sync.dma_start(out=wv_raw[g][:], in_=wv_rows[g])
         for q in range(2):
             nc.sync.dma_start(out=wo_raw[q][:], in_=wo_rows[q])
 
-        bo_all = consts.tile([P, H], BF16)
-        g_all = consts.tile([P, H], BF16)
-        r_all = consts.tile([P, H], F32)
-        one_minus_r = consts.tile([P, H], F32)
+        warm = consts.tile([P, 2], F32)
+        nc.vector.memset(warm[:], 0.0)
+        nc.scalar.activation(out=warm[:, 1:2], in_=warm[:, 0:1], func=ACT.Tanh)
 
-        def spread_vectors():
-            for half in range(2):
-                cols = slice(half * BANK, (half + 1) * BANK)
-                spread = [
-                    psum.tile([P, BANK], F32, name="spread%d" % n, tag="bank") for n in range(3)
-                ]
-                for n in range(3):
-                    nc.tensor.matmul(
-                        spread[n][:], lhsT=ones[:], rhs=vec_rows[:, n, cols], start=True, stop=True
-                    )
-                nc.scalar.copy(out=bo_all[:, cols], in_=spread[0][:])
-                nc.scalar.mul(out=g_all[:, cols], in_=spread[1][:], mul=SQRT_H)
-                nc.vector.tensor_scalar_add(out=r_all[:, cols], in0=spread[2][:], scalar1=TAU_EPS)
-            nc.vector.reciprocal(out=r_all[:], in_=r_all[:])
-            nc.gpsimd.tensor_scalar(
-                out=one_minus_r[:], in0=r_all[:], scalar1=-1.0, scalar2=1.0,
+        vec_cols = consts.tile([P, 40], F32)
+        r_cols = consts.tile([P, 8], F32)
+        omr_cols = consts.tile([P, 8], F32)
+        g_cols = consts.tile([P, 8], F32)
+        xin_bias = consts.tile([P, 8], F32)
+        bo_all = consts.tile([P, H], BF16)
+        omr_all = consts.tile([P, H], F32)
+
+        def make_vectors():
+            bank = psum.tile([P, P], BF16, name="vec_bank", tag="bank")
+            nc.tensor.transpose(bank[:], vec_rows[:], ident_bf[:])
+            nc.vector.tensor_copy(out=vec_cols[:], in_=bank[:, 0:40])
+            nc.vector.tensor_scalar_add(out=r_cols[:], in0=vec_cols[:, 16:24], scalar1=TAU_EPS)
+            nc.vector.tensor_scalar_mul(out=g_cols[:], in0=vec_cols[:, 8:16], scalar1=SQRT_H)
+            nc.vector.tensor_tensor(
+                out=xin_bias[:], in0=vec_cols[:, 24:32], in1=vec_cols[:, 32:40], op=ALU.add
+            )
+            nc.vector.reciprocal(out=r_cols[:], in_=r_cols[:])
+            nc.vector.tensor_scalar(
+                out=omr_cols[:], in0=r_cols[:], scalar1=-1.0, scalar2=1.0,
                 op0=ALU.mult, op1=ALU.add,
             )
+
+        def spread(columns, first, result):
+            for half in range(2):
+                bank = psum.tile([P, 4, P], F32, name="spread", tag="bank")
+                for j in range(4):
+                    col = first + 4 * half + j
+                    nc.tensor.transpose(
+                        bank[:, j, :], columns[:, col : col + 1].to_broadcast([P, P]), ident[:]
+                    )
+                nc.scalar.copy(
+                    out=result[:, half * BANK : (half + 1) * BANK],
+                    in_=bank[:].rearrange("p j n -> p (j n)"),
+                )
 
         def mx_operand(name, passes):
             codes = keep.tile([P, passes, 1024], U32, name=name + "_codes", align_bytes=64)
@@ -113,44 +126,60 @@ def tile_advancedliquidneuralnetwork_pb_kernel(
         x_mx = mx_operand("x", 1)
         win_mx = mx_operand("win", 1)
 
-        def transpose_four(word_blocks, grouped_words):
+        def transpose_bank(word_blocks, grouped_words, copy):
             bank = psum.tile([P, 4, P], F32, tag="bank")
             for n, block in enumerate(word_blocks):
                 nc.tensor.transpose(bank[:, n, :], block, ident[:])
-            nc.scalar.copy(out=grouped_words, in_=bank[:].rearrange("p (a u) r -> p a r u", u=2))
+            copy(out=grouped_words, in_=bank[:].rearrange("p (a u) r -> p a r u", u=2))
 
         def quantise(grouped, c, operand, cols):
             codes, scales = operand
             nc.vector.quantize_mx(
                 out=codes[:, c, cols].bitcast(FP8X4),
                 scales=scales[:, c, cols],
-                in_=grouped[:, c, :, :].rearrange("p r t -> p (r t)"),
+                in_=grouped.rearrange("p r t -> p (r t)"),
             )
 
-        def prepare_k1024(rows_raw, operand, chunk):
+        def unit_k1024(rows_raw, operand, chunk):
             words = rows_raw[:].bitcast(F32)
             grouped = stage.tile([P, 2, CHUNK, 4], BF16, tag="staged", align_bytes=64)
             grouped_words = grouped[:].bitcast(F32)
-            for i in range(TILES):
-                transpose_four(
+
+            def bank(i, copy):
+                transpose_bank(
                     [words[:, i, 256 * a + u : 256 * (a + 1) : 2] for a in range(2) for u in range(2)],
                     grouped_words[:, :, i * P : (i + 1) * P, :],
+                    copy,
                 )
-            for c in range(2):
-                quantise(grouped, c, operand, slice(chunk * CHUNK, (chunk + 1) * CHUNK))
 
-        def prepare_k512(rows_raw, operand):
+            def finish():
+                for c in range(2):
+                    quantise(
+                        grouped[:, c, :, :], c, operand, slice(chunk * CHUNK, (chunk + 1) * CHUNK)
+                    )
+
+            return bank, finish
+
+        def unit_k512(rows_raw, operand):
             words = rows_raw[:].bitcast(F32)
-            grouped = stage.tile([P, 1, 1024, 4], BF16, tag="staged", align_bytes=64)
+            grouped = stage.tile([P, 1024, 4], BF16, tag="staged", align_bytes=64)
             grouped_words = grouped[:].bitcast(F32)
-            for j in range(0, 8, 2):
-                transpose_four(
-                    [words[:, j + a, u:256:2] for a in range(2) for u in range(2)],
-                    grouped_words[:, 0, j * P : (j + 2) * P, :].rearrange(
+
+            def bank(i, copy):
+                transpose_bank(
+                    [words[:, 2 * i + a, u:256:2] for a in range(2) for u in range(2)],
+                    grouped_words[:, 2 * i * P : 2 * (i + 1) * P, :].rearrange(
                         "p (a r) u -> p a r u", a=2
                     ),
+                    copy,
                 )
-            quantise(grouped, 0, operand, slice(0, 1024))
+
+            def finish():
+                for half in range(2):
+                    cols = slice(half * CHUNK, (half + 1) * CHUNK)
+                    quantise(grouped[:, cols, :], 0, operand, cols)
+
+            return bank, finish
 
         def mx_matmul(acc, stationary, s_cols, moving, m_cols, passes):
             for c in range(passes):
@@ -167,23 +196,30 @@ def tile_advancedliquidneuralnetwork_pb_kernel(
         def tile_cols(n):
             return slice(n * P, (n + 1) * P)
 
+        v_grouped = {}
+
         def compute_v(n):
-            grouped = stage.tile([P, 2, P, 4], BF16, tag="v_grouped", bufs=3, align_bytes=64)
+            k, m = divmod(n, GROUP)
+            if m == 0:
+                v_grouped[k] = stage.tile(
+                    [P, 2, GCOLS, 4], BF16, name="v_grouped", tag="v_grouped", bufs=2, align_bytes=64
+                )
             for g in range(2):
                 bank = psum.tile([P, 4, P], F32, tag="bank")
                 for t in range(4):
                     mx_matmul(bank[:, t, :], wv_mx, tile_cols(4 * g + t), liq_mx, tile_cols(n), 2)
                 nc.vector.tensor_tensor(
-                    out=grouped[:, g, :, :],
+                    out=v_grouped[k][:, g, tile_cols(m), :],
                     in0=bank[:].rearrange("p t r -> p r t"),
                     in1=bv[:, 4 * g : 4 * g + 4].unsqueeze(1).to_broadcast([P, P, 4]),
                     op=ALU.add,
                 )
+
+        def quantise_v(k):
             for g in range(2):
-                quantise(grouped, g, v_mx, tile_cols(n))
+                quantise(v_grouped[k][:, g, :, :], g, v_mx, slice(k * GCOLS, (k + 1) * GCOLS))
 
         xin_t = keep.tile([P, 8, B], F32)
-        xin_bias = consts.tile([P, 8], F32)
 
         def compute_xin(q, features):
             cols = slice(q * CHUNK, (q + 1) * CHUNK)
@@ -195,82 +231,125 @@ def tile_advancedliquidneuralnetwork_pb_kernel(
                     bias=xin_bias[:, j : j + 1], scale=1.0,
                 )
 
-        residual, u_of, y_of, minus_mean_of, rstd_of, kept_of = {}, {}, {}, {}, {}, {}
         bank_cols = [slice(k * BANK, (k + 1) * BANK) for k in range(2)]
+        residual, kept, tanh_of, mean_of, squares_of = {}, {}, {}, {}, {}
 
-        def add_bias_to_liq(n):
+        def add_bias_to_liq(n, engine):
             q, i = divmod(n, TILES)
             residual[n] = work.tile([P, H], F32, name="residual", tag="residual", bufs=8)
-            nc.gpsimd.tensor_tensor(
+            engine.tensor_tensor(
                 out=residual[n][:], in0=liq_raw[q][:, i, :], in1=bo_all[:], op=ALU.add
             )
 
-        def statistics(n):
-            u = work.tile([P, H], F32, tag="u", bufs=2)
-            y = work.tile([P, H], F32, tag="y", bufs=4)
+        def keep_h(n):
+            q, i = divmod(n, TILES)
+            kept[n] = work.tile([P, H], F32, name="kept", tag="kept", bufs=6)
+            nc.gpsimd.tensor_tensor(
+                out=kept[n][:], in0=h_raw[q][:, i, :], in1=omr_all[:], op=ALU.mult
+            )
+
+        def add_att(n):
+            u = residual[n]
             sums = small.tile([P, 2], F32, tag="sums")
             for k, cols in enumerate(bank_cols):
                 att = psum.tile([P, BANK], F32, tag="bank")
                 mx_matmul(att[:], v_mx, tile_cols(n), wo_mx, cols, 2)
                 nc.vector.scalar_tensor_tensor(
-                    out=u[:, cols], in0=att[:], scalar=1.0, in1=residual[n][:, cols],
+                    out=u[:, cols], in0=att[:], scalar=1.0, in1=u[:, cols],
                     op0=ALU.mult, op1=ALU.add, accum_out=sums[:, k : k + 1],
                 )
-            minus_mean = small.tile([P, 1], F32, tag="minus_mean")
+            mean_of[n] = small.tile([P, 1], F32, name="minus_mean", tag="minus_mean")
             nc.vector.tensor_scalar(
-                out=minus_mean[:], in0=sums[:, 0:1], scalar1=sums[:, 1:2], scalar2=-1.0 / H,
+                out=mean_of[n][:], in0=sums[:, 0:1], scalar1=sums[:, 1:2], scalar2=-1.0 / H,
                 op0=ALU.add, op1=ALU.mult,
             )
+
+        def normalise(n):
+            u = residual[n]
             square_sum = small.tile([P, 1], F32, tag="square_sum")
+            squares = work.tile([P, H], BF16, tag="squares", bufs=1)
             nc.scalar.activation(
-                out=y[:], in_=u[:], func=ACT.Square, bias=minus_mean[:], scale=1.0,
+                out=squares[:], in_=u[:], func=ACT.Square, bias=mean_of[n][:], scale=1.0,
                 accum_out=square_sum[:],
             )
             rstd = small.tile([P, 1], F32, tag="rstd")
             nc.gpsimd.tensor_scalar_add(out=rstd[:], in0=square_sum[:], scalar1=H * LN_EPS)
             nc.gpsimd.tensor_tensor(out=rstd[:], in0=rstd[:], in1=minus_half[:], op=ALU.pow)
-            u_of[n], y_of[n], minus_mean_of[n], rstd_of[n] = u, y, minus_mean, rstd
-
-        def centre_and_scale(n):
-            q, i = divmod(n, TILES)
-            kept_of[n] = work.tile([P, H], F32, name="kept", tag="kept", bufs=2)
-            nc.gpsimd.tensor_tensor(
-                out=kept_of[n][:], in0=h_raw[q][:, i, :], in1=one_minus_r[:], op=ALU.mult
-            )
-            nc.vector.scalar_tensor_tensor(
-                out=y_of[n][:], in0=u_of[n][:], scalar=minus_mean_of[n][:], in1=g_all[:],
+            nc.gpsimd.tensor_scalar(
+                out=u[:], in0=u[:], scalar1=mean_of[n][:], scalar2=rstd[:],
                 op0=ALU.add, op1=ALU.mult,
             )
 
-        def add_xin_and_tanh(n):
-            y = y_of[n]
-            xin = [psum.tile([P, 4, P], F32, name="xin%d" % k, tag="bank") for k in range(2)]
-            for j in range(8):
-                nc.tensor.transpose(xin[j // 4][:, j % 4, :], xin_t[:, j, tile_cols(n)], ident[:])
-            for k, cols in enumerate(bank_cols):
-                nc.vector.scalar_tensor_tensor(
-                    out=y[:, cols], in0=y[:, cols], scalar=rstd_of[n][:],
-                    in1=xin[k][:].rearrange("p a r -> p (a r)"), op0=ALU.mult, op1=ALU.add,
+        def add_xin(k, half):
+            if half == 0:
+                tanh_of[k] = work.tile([P, 8, GCOLS], F32, name="tanh", tag="tanh", bufs=2)
+            t = tanh_of[k]
+            cols = slice(k * GCOLS, (k + 1) * GCOLS)
+            for pair in range(2):
+                bank = psum.tile([P, 2, GROUP, P], F32, tag="bank")
+                first = 4 * half + 2 * pair
+                for jj in range(2):
+                    for m in range(GROUP):
+                        nc.tensor.transpose(
+                            bank[:, jj, m, :], residual[GROUP * k + m][:, tile_cols(first + jj)],
+                            ident[:],
+                        )
+                for jj in range(2):
+                    j = first + jj
+                    nc.vector.scalar_tensor_tensor(
+                        out=t[:, j, :], in0=bank[:, jj, :, :].rearrange("p m r -> p (m r)"),
+                        scalar=g_cols[:, j : j + 1], in1=xin_t[:, j, cols],
+                        op0=ALU.mult, op1=ALU.add,
+                    )
+
+        def tanh_times_r(k, half):
+            t = tanh_of[k]
+            part = t[:, 4 * half : 4 * half + 4, :]
+            nc.scalar.activation(out=part, in_=part, func=ACT.Tanh)
+            for j in range(4 * half, 4 * half + 4):
+                nc.scalar.mul(out=t[:, j, :], in_=t[:, j, :], mul=r_cols[:, j : j + 1])
+
+        def finish(k, half):
+            t = tanh_of[k]
+            cols = bank_cols[half]
+            for m in range(GROUP):
+                n = GROUP * k + m
+                q, i = divmod(n, TILES)
+                bank = psum.tile([P, 4, P], F32, tag="bank")
+                for j in range(4):
+                    nc.tensor.transpose(bank[:, j, :], t[:, 4 * half + j, tile_cols(m)], ident[:])
+                nc.vector.tensor_tensor(
+                    out=kept[n][:, cols], in0=bank[:].rearrange("p j r -> p (j r)"),
+                    in1=kept[n][:, cols], op=ALU.add,
                 )
-            nc.scalar.activation(out=y[:], in_=y[:], func=ACT.Tanh)
+                nc.sync.dma_start(out=out_rows[q][:, i, cols], in_=kept[n][:, cols])
 
-        def times_r(n):
-            nc.vector.tensor_tensor(out=y_of[n][:], in0=y_of[n][:], in1=r_all[:], op=ALU.mult)
+        ctx.enter_context(tc.manual_schedule())
+        V, S = nc.vector.tensor_copy, nc.scalar.copy
 
-        def add_kept_and_store(n):
-            q, i = divmod(n, TILES)
-            y = y_of[n]
-            nc.vector.tensor_tensor(out=y[:], in0=y[:], in1=kept_of[n][:], op=ALU.add)
-            nc.sync.dma_start(out=out_rows[q][:, i, :], in_=y[:])
-
-        prepare_k1024(liq_raw[0], liq_mx, 0)
-        spread_vectors()
-        prepare_k1024(liq_raw[1], liq_mx, 1)
-        for n in range(8):
-            add_bias_to_liq(n)
-        for g in range(2):
-            prepare_k1024(wv_raw[g], wv_mx, g)
-
+        liq0, finish_liq0 = unit_k1024(liq_raw[0], liq_mx, 0)
+        liq0(0, V)
+        liq0(1, S)
+        liq0(2, V)
+        liq0(3, S)
+        make_vectors()
+        finish_liq0()
+        spread(vec_cols, 0, bo_all)
+        wv0, finish_wv0 = unit_k1024(wv_raw[0], wv_mx, 0)
+        wv0(0, S)
+        wv0(1, S)
+        wv0(2, S)
+        wv0(3, S)
+        add_bias_to_liq(0, nc.vector)
+        add_bias_to_liq(1, nc.vector)
+        finish_wv0()
+        wv1, finish_wv1 = unit_k1024(wv_raw[1], wv_mx, 1)
+        wv1(0, S)
+        wv1(1, S)
+        wv1(2, S)
+        wv1(3, S)
+        add_bias_to_liq(2, nc.vector)
+        finish_wv1()
         win_raw = raw.tile([P, 8, IN], BF16, tag="raw")
         x_raw = raw.tile([P, 8, IN], BF16, tag="raw")
         nc.sync.dma_start(out=win_raw[:], in_=W_in.rearrange("(j p) k -> p j k", p=P))
@@ -278,36 +357,106 @@ def tile_advancedliquidneuralnetwork_pb_kernel(
             out=x_raw[:].rearrange("p (q i) k -> p q i k", q=2),
             in_=x.rearrange("(q p i) k -> p q i k", q=2, i=TILES),
         )
-        beta_t = consts.tile([P, 8], BF16)
-        bin_t = consts.tile([P, 8], BF16)
-        with nc.allow_non_contiguous_dma(reason="two vectors of 1024, one element a partition"):
-            nc.sync.dma_start(out=beta_t[:], in_=beta_att.rearrange("(j p) -> p j", p=P))
-            nc.sync.dma_start(out=bin_t[:], in_=b_in.rearrange("(j p) -> p j", p=P))
-
-        prepare_k1024(wo_raw[0], wo_mx, 0)
+        nc.sync.dma_start(out=liq_raw[1][:], in_=liq_rows[1])
+        wo0, finish_wo0 = unit_k1024(wo_raw[0], wo_mx, 0)
+        wo0(0, S)
+        wo0(1, V)
+        wo0(2, S)
+        wo0(3, S)
+        finish_wo0()
         compute_v(0)
+        wo1, finish_wo1 = unit_k1024(wo_raw[1], wo_mx, 1)
+        wo1(0, S)
+        wo1(1, V)
+        wo1(2, S)
+        wo1(3, S)
+        finish_wo1()
         compute_v(1)
-        prepare_k1024(wo_raw[1], wo_mx, 1)
+        quantise_v(0)
         h_raw = [raw.tile([P, TILES, H], BF16, name="h_raw%d" % q, tag="raw") for q in range(2)]
         for q in range(2):
             nc.sync.dma_start(out=h_raw[q][:], in_=h_rows[q])
+        win, finish_win = unit_k512(win_raw, win_mx)
+        win(0, S)
+        win(1, S)
+        win(2, S)
+        win(3, S)
+        add_att(0)
+        finish_win()
+        add_att(1)
+        normalise(0)
+        normalise(1)
+        xs, finish_x = unit_k512(x_raw, x_mx)
+        xs(0, S)
+        xs(1, S)
+        xs(2, S)
+        xs(3, S)
         compute_v(2)
+        finish_x()
         compute_v(3)
-        prepare_k512(win_raw, win_mx)
-        prepare_k512(x_raw, x_mx)
-        nc.vector.tensor_tensor(out=xin_bias[:], in0=beta_t[:], in1=bin_t[:], op=ALU.add)
-
-        for n in range(8 + 2):
-            if n < 8:
-                statistics(n)
-            if n < TILES:
-                compute_xin(n // 2, range(4 * (n % 2), 4 * (n % 2) + 4))
-                compute_v(n + TILES)
-            if 0 <= n - 1 < 8:
-                centre_and_scale(n - 1)
-            if 0 <= n - 2 < 8:
-                times_r(n - 2)
-            if 0 <= n - 1 < 8:
-                add_xin_and_tanh(n - 1)
-            if 0 <= n - 2 < 8:
-                add_kept_and_store(n - 2)
+        quantise_v(1)
+        add_bias_to_liq(3, nc.vector)
+        spread(omr_cols, 0, omr_all)
+        liq1, finish_liq1 = unit_k1024(liq_raw[1], liq_mx, 1)
+        liq1(0, S)
+        liq1(1, S)
+        liq1(2, S)
+        liq1(3, S)
+        finish_liq1()
+        compute_xin(0, range(0, 8))
+        add_att(2)
+        add_att(3)
+        normalise(2)
+        normalise(3)
+        compute_v(4)
+        compute_v(5)
+        quantise_v(2)
+        add_bias_to_liq(4, nc.gpsimd)
+        add_bias_to_liq(5, nc.gpsimd)
+        keep_h(0)
+        keep_h(1)
+        add_xin(0, 0)
+        tanh_times_r(0, 0)
+        add_xin(0, 1)
+        tanh_times_r(0, 1)
+        compute_xin(1, range(0, 4))
+        add_att(4)
+        add_att(5)
+        normalise(4)
+        normalise(5)
+        compute_v(6)
+        compute_v(7)
+        quantise_v(3)
+        add_bias_to_liq(6, nc.gpsimd)
+        add_bias_to_liq(7, nc.gpsimd)
+        keep_h(2)
+        keep_h(3)
+        add_xin(1, 0)
+        tanh_times_r(1, 0)
+        add_xin(1, 1)
+        tanh_times_r(1, 1)
+        finish(0, 0)
+        finish(0, 1)
+        compute_xin(1, range(4, 8))
+        add_att(6)
+        add_att(7)
+        normalise(6)
+        normalise(7)
+        keep_h(4)
+        keep_h(5)
+        add_xin(2, 0)
+        tanh_times_r(2, 0)
+        add_xin(2, 1)
+        tanh_times_r(2, 1)
+        finish(1, 0)
+        finish(1, 1)
+        keep_h(6)
+        keep_h(7)
+        add_xin(3, 0)
+        tanh_times_r(3, 0)
+        finish(2, 0)
+        add_xin(3, 1)
+        tanh_times_r(3, 1)
+        finish(2, 1)
+        finish(3, 0)
+        finish(3, 1)

@@ -55,8 +55,6 @@ def tile_advancedliquidneuralnetwork_pb_kernel(
         nc.vector.memset(minus_half[:], -0.5)
 
         liq_raw = [keep.tile([P, TILES, H], BF16, name="liq_raw%d" % q) for q in range(2)]
-        wv_raw = [raw.tile([P, TILES, H], BF16, name="wv_raw%d" % g, tag="raw") for g in range(2)]
-        wo_raw = [raw.tile([P, TILES, H], BF16, name="wo_raw%d" % q, tag="raw") for q in range(2)]
         for n, vector in enumerate((b_o, g_att, tau, beta_att, b_in)):
             nc.sync.dma_start(
                 out=vec_rows[8 * n : 8 * n + 8, :], in_=vector.rearrange("(j p) -> j p", p=P)
@@ -66,13 +64,6 @@ def tile_advancedliquidneuralnetwork_pb_kernel(
             out=bv[:].rearrange("p (g t) -> p g t", t=4),
             in_=b_v.rearrange("(g p t) -> p g t", p=P, t=4),
         )
-
-        for i in range(0, TILES, 2):
-            nc.sync.dma_start(out=liq_raw[0][:, i : i + 2, :], in_=liq_rows[0][:, i : i + 2, :])
-        for g in range(2):
-            nc.sync.dma_start(out=wv_raw[g][:], in_=wv_rows[g])
-        for q in range(2):
-            nc.sync.dma_start(out=wo_raw[q][:], in_=wo_rows[q])
 
         warm = consts.tile([P, 2], F32)
         nc.vector.memset(warm[:], 0.0)
@@ -114,17 +105,17 @@ def tile_advancedliquidneuralnetwork_pb_kernel(
                     in_=bank[:].rearrange("p j n -> p (j n)"),
                 )
 
-        def mx_operand(name, passes):
-            codes = keep.tile([P, passes, 1024], U32, name=name + "_codes", align_bytes=64)
-            scales = keep.tile([P, passes, 1024], U8, name=name + "_scales", align_bytes=64)
+        def mx_operand(name, sets, passes, rows):
+            codes = keep.tile([P, sets, passes, rows], U32, name=name + "_codes", align_bytes=64)
+            scales = keep.tile([P, sets, passes, rows], U8, name=name + "_scales", align_bytes=64)
             return codes, scales
 
-        liq_mx = mx_operand("liq", 2)
-        wv_mx = mx_operand("wv", 2)
-        v_mx = mx_operand("v", 2)
-        wo_mx = mx_operand("wo", 2)
-        x_mx = mx_operand("x", 1)
-        win_mx = mx_operand("win", 1)
+        liq_mx = mx_operand("liq", 2, 2, CHUNK)
+        wv_mx = mx_operand("wv", 2, 2, CHUNK)
+        v_mx = mx_operand("v", 4, 2, GCOLS)
+        wo_mx = mx_operand("wo", 2, 2, CHUNK)
+        x_mx = mx_operand("x", 2, 1, CHUNK)
+        win_mx = mx_operand("win", 2, 1, CHUNK)
 
         def transpose_bank(word_blocks, grouped_words, copy):
             bank = psum.tile([P, 4, P], F32, tag="bank")
@@ -132,12 +123,12 @@ def tile_advancedliquidneuralnetwork_pb_kernel(
                 nc.tensor.transpose(bank[:, n, :], block, ident[:])
             copy(out=grouped_words, in_=bank[:].rearrange("p (a u) r -> p a r u", u=2))
 
-        def quantise(grouped, c, operand, cols):
+        def quantise(grouped, operand, s):
             codes, scales = operand
             nc.vector.quantize_mx(
-                out=codes[:, c, cols].bitcast(FP8X4),
-                scales=scales[:, c, cols],
-                in_=grouped.rearrange("p r t -> p (r t)"),
+                out=codes[:, s, :, :].rearrange("p c r -> p (c r)").bitcast(FP8X4),
+                scales=scales[:, s, :, :].rearrange("p c r -> p (c r)"),
+                in_=grouped.rearrange("p c r t -> p (c r t)"),
             )
 
         def unit_k1024(rows_raw, operand, chunk):
@@ -153,42 +144,41 @@ def tile_advancedliquidneuralnetwork_pb_kernel(
                 )
 
             def finish():
-                for c in range(2):
-                    quantise(
-                        grouped[:, c, :, :], c, operand, slice(chunk * CHUNK, (chunk + 1) * CHUNK)
-                    )
+                quantise(grouped[:], operand, chunk)
 
             return bank, finish
 
         def unit_k512(rows_raw, operand):
             words = rows_raw[:].bitcast(F32)
-            grouped = stage.tile([P, 1024, 4], BF16, tag="staged", align_bytes=64)
+            grouped = stage.tile([P, 2, CHUNK, 4], BF16, tag="staged", align_bytes=64)
             grouped_words = grouped[:].bitcast(F32)
 
             def bank(i, copy):
                 transpose_bank(
                     [words[:, 2 * i + a, u:256:2] for a in range(2) for u in range(2)],
-                    grouped_words[:, 2 * i * P : 2 * (i + 1) * P, :].rearrange(
+                    grouped_words[:, i // 2, GCOLS * (i % 2) : GCOLS * (i % 2 + 1), :].rearrange(
                         "p (a r) u -> p a r u", a=2
                     ),
                     copy,
                 )
 
             def finish():
-                for half in range(2):
-                    cols = slice(half * CHUNK, (half + 1) * CHUNK)
-                    quantise(grouped[:, cols, :], 0, operand, cols)
+                for s in range(2):
+                    quantise(grouped[:, s : s + 1, :, :], operand, s)
 
             return bank, finish
 
-        def mx_matmul(acc, stationary, s_cols, moving, m_cols, passes):
+        def mx_matmul(acc, stationary, moving):
+            (s_codes, s_scales), s_set, s_cols = stationary
+            (m_codes, m_scales), m_set, m_cols = moving
+            passes = s_codes.shape[2]
             for c in range(passes):
                 nc.tensor.matmul_mx(
                     out=acc,
-                    lhsT=stationary[0][:, c, s_cols].bitcast(FP8X4),
-                    lhsT_scale=stationary[1][:, c, s_cols],
-                    rhs=moving[0][:, c, m_cols].bitcast(FP8X4),
-                    rhs_scale=moving[1][:, c, m_cols],
+                    lhsT=s_codes[:, s_set, c, s_cols].bitcast(FP8X4),
+                    lhsT_scale=s_scales[:, s_set, c, s_cols],
+                    rhs=m_codes[:, m_set, c, m_cols].bitcast(FP8X4),
+                    rhs_scale=m_scales[:, m_set, c, m_cols],
                     start=(c == 0),
                     stop=(c == passes - 1),
                 )
@@ -207,7 +197,10 @@ def tile_advancedliquidneuralnetwork_pb_kernel(
             for g in range(2):
                 bank = psum.tile([P, 4, P], F32, tag="bank")
                 for t in range(4):
-                    mx_matmul(bank[:, t, :], wv_mx, tile_cols(4 * g + t), liq_mx, tile_cols(n), 2)
+                    mx_matmul(
+                        bank[:, t, :], (wv_mx, g, tile_cols(t)),
+                        (liq_mx, n // TILES, tile_cols(n % TILES)),
+                    )
                 nc.vector.tensor_tensor(
                     out=v_grouped[k][:, g, tile_cols(m), :],
                     in0=bank[:].rearrange("p t r -> p r t"),
@@ -216,8 +209,7 @@ def tile_advancedliquidneuralnetwork_pb_kernel(
                 )
 
         def quantise_v(k):
-            for g in range(2):
-                quantise(v_grouped[k][:, g, :, :], g, v_mx, slice(k * GCOLS, (k + 1) * GCOLS))
+            quantise(v_grouped[k][:], v_mx, k)
 
         xin_t = keep.tile([P, 8, B], F32)
 
@@ -225,7 +217,9 @@ def tile_advancedliquidneuralnetwork_pb_kernel(
             cols = slice(q * CHUNK, (q + 1) * CHUNK)
             for j in features:
                 bank = psum.tile([P, BANK], F32, tag="bank")
-                mx_matmul(bank[:], win_mx, tile_cols(j), x_mx, cols, 1)
+                mx_matmul(
+                    bank[:], (win_mx, j // TILES, tile_cols(j % TILES)), (x_mx, q, slice(0, CHUNK))
+                )
                 nc.scalar.activation(
                     out=xin_t[:, j, cols], in_=bank[:], func=ACT.Identity,
                     bias=xin_bias[:, j : j + 1], scale=1.0,
@@ -253,7 +247,9 @@ def tile_advancedliquidneuralnetwork_pb_kernel(
             sums = small.tile([P, 2], F32, tag="sums")
             for k, cols in enumerate(bank_cols):
                 att = psum.tile([P, BANK], F32, tag="bank")
-                mx_matmul(att[:], v_mx, tile_cols(n), wo_mx, cols, 2)
+                mx_matmul(
+                    att[:], (v_mx, n // GROUP, tile_cols(n % GROUP)), (wo_mx, k, slice(0, CHUNK))
+                )
                 nc.vector.scalar_tensor_tensor(
                     out=u[:, cols], in0=att[:], scalar=1.0, in1=u[:, cols],
                     op0=ALU.mult, op1=ALU.add, accum_out=sums[:, k : k + 1],
@@ -324,9 +320,16 @@ def tile_advancedliquidneuralnetwork_pb_kernel(
                 )
                 nc.sync.dma_start(out=out_rows[q][:, i, cols], in_=kept[n][:, cols])
 
-        ctx.enter_context(tc.manual_schedule())
         V, S = nc.vector.tensor_copy, nc.scalar.copy
 
+        for i in range(0, TILES, 2):
+            nc.sync.dma_start(out=liq_raw[0][:, i : i + 2, :], in_=liq_rows[0][:, i : i + 2, :])
+        wv_raw = [raw.tile([P, TILES, H], BF16, name="wv_raw%d" % g, tag="raw") for g in range(2)]
+        for g in range(2):
+            nc.sync.dma_start(out=wv_raw[g][:], in_=wv_rows[g])
+        wo_raw = [raw.tile([P, TILES, H], BF16, name="wo_raw%d" % q, tag="raw") for q in range(2)]
+        for q in range(2):
+            nc.sync.dma_start(out=wo_raw[q][:], in_=wo_rows[q])
         liq0, finish_liq0 = unit_k1024(liq_raw[0], liq_mx, 0)
         liq0(0, V)
         liq0(1, S)
@@ -348,15 +351,13 @@ def tile_advancedliquidneuralnetwork_pb_kernel(
         wv1(1, S)
         wv1(2, S)
         wv1(3, S)
-        add_bias_to_liq(2, nc.vector)
         finish_wv1()
         win_raw = raw.tile([P, 8, IN], BF16, tag="raw")
-        x_raw = raw.tile([P, 8, IN], BF16, tag="raw")
         nc.sync.dma_start(out=win_raw[:], in_=W_in.rearrange("(j p) k -> p j k", p=P))
-        nc.sync.dma_start(
-            out=x_raw[:].rearrange("p (q i) k -> p q i k", q=2),
-            in_=x.rearrange("(q p i) k -> p q i k", q=2, i=TILES),
-        )
+        x_raw = raw.tile([P, 8, IN], BF16, tag="raw")
+        x_rows = x.rearrange("(q p i) k -> q p i k", q=2, i=TILES)
+        for q in range(2):
+            nc.sync.dma_start(out=x_raw[:, TILES * q : TILES * (q + 1), :], in_=x_rows[q])
         nc.sync.dma_start(out=liq_raw[1][:], in_=liq_rows[1])
         wo0, finish_wo0 = unit_k1024(wo_raw[0], wo_mx, 0)
         wo0(0, S)
@@ -386,16 +387,18 @@ def tile_advancedliquidneuralnetwork_pb_kernel(
         add_att(1)
         normalise(0)
         normalise(1)
-        xs, finish_x = unit_k512(x_raw, x_mx)
+        add_bias_to_liq(2, nc.vector)
+        xs, finish_xs = unit_k512(x_raw, x_mx)
         xs(0, S)
         xs(1, S)
         xs(2, S)
         xs(3, S)
         compute_v(2)
-        finish_x()
+        add_bias_to_liq(3, nc.vector)
+        finish_xs()
         compute_v(3)
         quantise_v(1)
-        add_bias_to_liq(3, nc.vector)
+        add_bias_to_liq(4, nc.vector)
         spread(omr_cols, 0, omr_all)
         liq1, finish_liq1 = unit_k1024(liq_raw[1], liq_mx, 1)
         liq1(0, S)
@@ -411,14 +414,14 @@ def tile_advancedliquidneuralnetwork_pb_kernel(
         compute_v(4)
         compute_v(5)
         quantise_v(2)
-        add_bias_to_liq(4, nc.gpsimd)
-        add_bias_to_liq(5, nc.gpsimd)
         keep_h(0)
         keep_h(1)
+        keep_h(2)
         add_xin(0, 0)
         tanh_times_r(0, 0)
         add_xin(0, 1)
         tanh_times_r(0, 1)
+        add_bias_to_liq(5, nc.vector)
         compute_xin(1, range(0, 4))
         add_att(4)
         add_att(5)
@@ -427,14 +430,14 @@ def tile_advancedliquidneuralnetwork_pb_kernel(
         compute_v(6)
         compute_v(7)
         quantise_v(3)
-        add_bias_to_liq(6, nc.gpsimd)
-        add_bias_to_liq(7, nc.gpsimd)
-        keep_h(2)
         keep_h(3)
+        keep_h(4)
         add_xin(1, 0)
         tanh_times_r(1, 0)
         add_xin(1, 1)
         tanh_times_r(1, 1)
+        add_bias_to_liq(6, nc.vector)
+        add_bias_to_liq(7, nc.vector)
         finish(0, 0)
         finish(0, 1)
         compute_xin(1, range(4, 8))
@@ -442,7 +445,6 @@ def tile_advancedliquidneuralnetwork_pb_kernel(
         add_att(7)
         normalise(6)
         normalise(7)
-        keep_h(4)
         keep_h(5)
         add_xin(2, 0)
         tanh_times_r(2, 0)

@@ -226,21 +226,24 @@ def tile_advancedliquidneuralnetwork_pb_kernel(
                 )
 
         bank_cols = [slice(k * BANK, (k + 1) * BANK) for k in range(2)]
-        residual, kept, tanh_of, mean_of, squares_of = {}, {}, {}, {}, {}
+        residual, kept, tanh_of, sums_of = {}, {}, {}, {}
 
         def add_bias_to_liq(n, engine):
             q, i = divmod(n, TILES)
             residual[n] = work.tile([P, H], F32, name="residual", tag="residual", bufs=8)
-            engine.tensor_tensor(
-                out=residual[n][:], in0=liq_raw[q][:, i, :], in1=bo_all[:], op=ALU.add
-            )
+            for cols in bank_cols if engine is nc.gpsimd else (slice(0, H),):
+                engine.tensor_tensor(
+                    out=residual[n][:, cols], in0=liq_raw[q][:, i, cols], in1=bo_all[:, cols],
+                    op=ALU.add,
+                )
 
         def keep_h(n):
             q, i = divmod(n, TILES)
             kept[n] = work.tile([P, H], F32, name="kept", tag="kept", bufs=6)
-            nc.gpsimd.tensor_tensor(
-                out=kept[n][:], in0=h_raw[q][:, i, :], in1=omr_all[:], op=ALU.mult
-            )
+            for cols in bank_cols:
+                nc.gpsimd.tensor_tensor(
+                    out=kept[n][:, cols], in0=h_raw[q][:, i, cols], in1=omr_all[:, cols], op=ALU.mult
+                )
 
         def add_att(n):
             u = residual[n]
@@ -254,25 +257,27 @@ def tile_advancedliquidneuralnetwork_pb_kernel(
                     out=u[:, cols], in0=att[:], scalar=1.0, in1=u[:, cols],
                     op0=ALU.mult, op1=ALU.add, accum_out=sums[:, k : k + 1],
                 )
-            mean_of[n] = small.tile([P, 1], F32, name="minus_mean", tag="minus_mean")
-            nc.vector.tensor_scalar(
-                out=mean_of[n][:], in0=sums[:, 0:1], scalar1=sums[:, 1:2], scalar2=-1.0 / H,
-                op0=ALU.add, op1=ALU.mult,
-            )
+            sums_of[n] = sums
 
         def normalise(n):
             u = residual[n]
+            minus_mean = small.tile([P, 1], F32, tag="minus_mean")
+            scaled_sums = small.tile([P, 2], F32, tag="scaled_sums")
+            nc.scalar.activation(
+                out=scaled_sums[:], in_=sums_of[n][:], func=ACT.Identity, scale=-1.0 / H,
+                accum_out=minus_mean[:],
+            )
             square_sum = small.tile([P, 1], F32, tag="square_sum")
             squares = work.tile([P, H], BF16, tag="squares", bufs=1)
             nc.scalar.activation(
-                out=squares[:], in_=u[:], func=ACT.Square, bias=mean_of[n][:], scale=1.0,
+                out=squares[:], in_=u[:], func=ACT.Square, bias=minus_mean[:], scale=1.0,
                 accum_out=square_sum[:],
             )
             rstd = small.tile([P, 1], F32, tag="rstd")
             nc.gpsimd.tensor_scalar_add(out=rstd[:], in0=square_sum[:], scalar1=H * LN_EPS)
             nc.gpsimd.tensor_tensor(out=rstd[:], in0=rstd[:], in1=minus_half[:], op=ALU.pow)
             nc.gpsimd.tensor_scalar(
-                out=u[:], in0=u[:], scalar1=mean_of[n][:], scalar2=rstd[:],
+                out=u[:], in0=u[:], scalar1=minus_mean[:], scalar2=rstd[:],
                 op0=ALU.add, op1=ALU.mult,
             )
 
@@ -361,14 +366,14 @@ def tile_advancedliquidneuralnetwork_pb_kernel(
         nc.sync.dma_start(out=liq_raw[1][:], in_=liq_rows[1])
         wo0, finish_wo0 = unit_k1024(wo_raw[0], wo_mx, 0)
         wo0(0, S)
-        wo0(1, V)
+        wo0(1, S)
         wo0(2, S)
         wo0(3, S)
         finish_wo0()
         compute_v(0)
         wo1, finish_wo1 = unit_k1024(wo_raw[1], wo_mx, 1)
         wo1(0, S)
-        wo1(1, V)
+        wo1(1, S)
         wo1(2, S)
         wo1(3, S)
         finish_wo1()
@@ -398,7 +403,6 @@ def tile_advancedliquidneuralnetwork_pb_kernel(
         finish_xs()
         compute_v(3)
         quantise_v(1)
-        add_bias_to_liq(4, nc.vector)
         spread(omr_cols, 0, omr_all)
         liq1, finish_liq1 = unit_k1024(liq_raw[1], liq_mx, 1)
         liq1(0, S)
@@ -411,33 +415,33 @@ def tile_advancedliquidneuralnetwork_pb_kernel(
         add_att(3)
         normalise(2)
         normalise(3)
+        add_bias_to_liq(4, nc.gpsimd)
         compute_v(4)
         compute_v(5)
         quantise_v(2)
+        add_bias_to_liq(5, nc.gpsimd)
         keep_h(0)
         keep_h(1)
-        keep_h(2)
         add_xin(0, 0)
         tanh_times_r(0, 0)
         add_xin(0, 1)
         tanh_times_r(0, 1)
-        add_bias_to_liq(5, nc.vector)
         compute_xin(1, range(0, 4))
         add_att(4)
         add_att(5)
         normalise(4)
         normalise(5)
+        add_bias_to_liq(6, nc.gpsimd)
+        add_bias_to_liq(7, nc.gpsimd)
         compute_v(6)
         compute_v(7)
         quantise_v(3)
+        keep_h(2)
         keep_h(3)
-        keep_h(4)
         add_xin(1, 0)
         tanh_times_r(1, 0)
         add_xin(1, 1)
         tanh_times_r(1, 1)
-        add_bias_to_liq(6, nc.vector)
-        add_bias_to_liq(7, nc.vector)
         finish(0, 0)
         finish(0, 1)
         compute_xin(1, range(4, 8))
@@ -445,6 +449,7 @@ def tile_advancedliquidneuralnetwork_pb_kernel(
         add_att(7)
         normalise(6)
         normalise(7)
+        keep_h(4)
         keep_h(5)
         add_xin(2, 0)
         tanh_times_r(2, 0)

@@ -281,14 +281,13 @@ def tile_advancedliquidneuralnetwork_pb_kernel(
                 op0=ALU.add, op1=ALU.mult,
             )
 
-        def add_xin(k, half):
-            if half == 0:
+        def add_xin(k, blocks):
+            if k not in tanh_of:
                 tanh_of[k] = work.tile([P, 8, GCOLS], F32, name="tanh", tag="tanh", bufs=2)
             t = tanh_of[k]
             cols = slice(k * GCOLS, (k + 1) * GCOLS)
-            for pair in range(2):
+            for first in blocks[::2]:
                 bank = psum.tile([P, 2, GROUP, P], F32, tag="bank")
-                first = 4 * half + 2 * pair
                 for jj in range(2):
                     for m in range(GROUP):
                         nc.tensor.transpose(
@@ -303,12 +302,18 @@ def tile_advancedliquidneuralnetwork_pb_kernel(
                         op0=ALU.mult, op1=ALU.add,
                     )
 
-        def tanh_times_r(k, half):
+        def tanh_times_r(k, blocks, multiply):
             t = tanh_of[k]
-            part = t[:, 4 * half : 4 * half + 4, :]
+            part = t[:, blocks[0] : blocks[-1] + 1, :]
             nc.scalar.activation(out=part, in_=part, func=ACT.Tanh)
-            for j in range(4 * half, 4 * half + 4):
-                nc.scalar.mul(out=t[:, j, :], in_=t[:, j, :], mul=r_cols[:, j : j + 1])
+            for j in blocks:
+                multiply(t[:, j, :], r_cols[:, j : j + 1])
+
+        def multiply_on_scalar(values, factor):
+            nc.scalar.mul(out=values, in_=values, mul=factor)
+
+        def multiply_on_vector(values, factor):
+            nc.vector.tensor_scalar_mul(out=values, in0=values, scalar1=factor)
 
         def finish(k, half):
             t = tanh_of[k]
@@ -325,6 +330,7 @@ def tile_advancedliquidneuralnetwork_pb_kernel(
                 )
                 nc.sync.dma_start(out=out_rows[q][:, i, cols], in_=kept[n][:, cols])
 
+        ctx.enter_context(tc.manual_schedule(engines={mybir.EngineType.Pool}))
         V, S = nc.vector.tensor_copy, nc.scalar.copy
 
         for i in range(0, TILES, 2):
@@ -341,61 +347,63 @@ def tile_advancedliquidneuralnetwork_pb_kernel(
         liq0(2, V)
         liq0(3, S)
         make_vectors()
-        finish_liq0()
         spread(vec_cols, 0, bo_all)
+        finish_liq0()
         wv0, finish_wv0 = unit_k1024(wv_raw[0], wv_mx, 0)
-        wv0(0, S)
+        wv0(0, V)
         wv0(1, S)
-        wv0(2, S)
+        wv0(2, V)
         wv0(3, S)
         add_bias_to_liq(0, nc.vector)
         add_bias_to_liq(1, nc.vector)
         finish_wv0()
         wv1, finish_wv1 = unit_k1024(wv_raw[1], wv_mx, 1)
-        wv1(0, S)
+        wv1(0, V)
         wv1(1, S)
         wv1(2, S)
         wv1(3, S)
         finish_wv1()
+        nc.sync.dma_start(out=liq_raw[1][:], in_=liq_rows[1])
         win_raw = raw.tile([P, 8, IN], BF16, tag="raw")
         nc.sync.dma_start(out=win_raw[:], in_=W_in.rearrange("(j p) k -> p j k", p=P))
         x_raw = raw.tile([P, 8, IN], BF16, tag="raw")
         x_rows = x.rearrange("(q p i) k -> q p i k", q=2, i=TILES)
         for q in range(2):
             nc.sync.dma_start(out=x_raw[:, TILES * q : TILES * (q + 1), :], in_=x_rows[q])
-        nc.sync.dma_start(out=liq_raw[1][:], in_=liq_rows[1])
         wo0, finish_wo0 = unit_k1024(wo_raw[0], wo_mx, 0)
         wo0(0, S)
         wo0(1, S)
         wo0(2, S)
         wo0(3, S)
-        finish_wo0()
         compute_v(0)
+        add_bias_to_liq(2, nc.vector)
+        finish_wo0()
         wo1, finish_wo1 = unit_k1024(wo_raw[1], wo_mx, 1)
         wo1(0, S)
         wo1(1, S)
         wo1(2, S)
         wo1(3, S)
-        finish_wo1()
         compute_v(1)
+        finish_wo1()
         quantise_v(0)
         h_raw = [raw.tile([P, TILES, H], BF16, name="h_raw%d" % q, tag="raw") for q in range(2)]
         for q in range(2):
             nc.sync.dma_start(out=h_raw[q][:], in_=h_rows[q])
+        add_bias_to_liq(4, nc.gpsimd)
+        add_bias_to_liq(5, nc.gpsimd)
         win, finish_win = unit_k512(win_raw, win_mx)
         win(0, S)
         win(1, S)
         win(2, S)
         win(3, S)
-        add_att(0)
-        finish_win()
-        add_att(1)
-        normalise(0)
-        normalise(1)
-        add_bias_to_liq(2, nc.vector)
         xs, finish_xs = unit_k512(x_raw, x_mx)
         xs(0, S)
         xs(1, S)
+        finish_win()
+        add_att(0)
+        add_att(1)
+        normalise(0)
+        normalise(1)
         xs(2, S)
         xs(3, S)
         compute_v(2)
@@ -403,6 +411,8 @@ def tile_advancedliquidneuralnetwork_pb_kernel(
         finish_xs()
         compute_v(3)
         quantise_v(1)
+        add_bias_to_liq(6, nc.gpsimd)
+        add_bias_to_liq(7, nc.gpsimd)
         spread(omr_cols, 0, omr_all)
         liq1, finish_liq1 = unit_k1024(liq_raw[1], liq_mx, 1)
         liq1(0, S)
@@ -411,37 +421,35 @@ def tile_advancedliquidneuralnetwork_pb_kernel(
         liq1(3, S)
         finish_liq1()
         compute_xin(0, range(0, 8))
+        keep_h(0)
         add_att(2)
         add_att(3)
         normalise(2)
         normalise(3)
-        add_bias_to_liq(4, nc.gpsimd)
+        keep_h(1)
         compute_v(4)
         compute_v(5)
         quantise_v(2)
-        add_bias_to_liq(5, nc.gpsimd)
-        keep_h(0)
-        keep_h(1)
-        add_xin(0, 0)
-        tanh_times_r(0, 0)
-        add_xin(0, 1)
-        tanh_times_r(0, 1)
+        add_xin(0, range(0, 4))
+        tanh_times_r(0, range(0, 4), multiply_on_scalar)
+        add_xin(0, range(4, 8))
+        tanh_times_r(0, range(4, 8), multiply_on_scalar)
         compute_xin(1, range(0, 4))
+        keep_h(2)
+        keep_h(3)
         add_att(4)
         add_att(5)
         normalise(4)
         normalise(5)
-        add_bias_to_liq(6, nc.gpsimd)
-        add_bias_to_liq(7, nc.gpsimd)
         compute_v(6)
         compute_v(7)
         quantise_v(3)
-        keep_h(2)
-        keep_h(3)
-        add_xin(1, 0)
-        tanh_times_r(1, 0)
-        add_xin(1, 1)
-        tanh_times_r(1, 1)
+        add_xin(1, range(0, 4))
+        tanh_times_r(1, range(0, 4), multiply_on_scalar)
+        add_xin(1, range(4, 8))
+        tanh_times_r(1, range(4, 8), multiply_on_scalar)
+        keep_h(4)
+        keep_h(5)
         finish(0, 0)
         finish(0, 1)
         compute_xin(1, range(4, 8))
@@ -449,21 +457,23 @@ def tile_advancedliquidneuralnetwork_pb_kernel(
         add_att(7)
         normalise(6)
         normalise(7)
-        keep_h(4)
-        keep_h(5)
-        add_xin(2, 0)
-        tanh_times_r(2, 0)
-        add_xin(2, 1)
-        tanh_times_r(2, 1)
+        add_xin(2, range(0, 4))
+        tanh_times_r(2, range(0, 4), multiply_on_scalar)
+        add_xin(2, range(4, 8))
+        tanh_times_r(2, range(4, 8), multiply_on_scalar)
         finish(1, 0)
         finish(1, 1)
         keep_h(6)
         keep_h(7)
-        add_xin(3, 0)
-        tanh_times_r(3, 0)
+        add_xin(3, range(0, 2))
+        tanh_times_r(3, range(0, 2), multiply_on_scalar)
+        add_xin(3, range(2, 4))
+        tanh_times_r(3, range(2, 4), multiply_on_vector)
         finish(2, 0)
-        add_xin(3, 1)
-        tanh_times_r(3, 1)
+        add_xin(3, range(4, 6))
+        tanh_times_r(3, range(4, 6), multiply_on_scalar)
+        add_xin(3, range(6, 8))
+        tanh_times_r(3, range(6, 8), multiply_on_vector)
         finish(2, 1)
         finish(3, 0)
         finish(3, 1)

@@ -259,7 +259,7 @@ def tile_advancedliquidneuralnetwork_pb_kernel(
                 )
             sums_of[n] = sums
 
-        def normalise(n):
+        def normalise(n, engine):
             u = residual[n]
             minus_mean = small.tile([P, 1], F32, tag="minus_mean")
             scaled_sums = small.tile([P, 2], F32, tag="scaled_sums")
@@ -276,7 +276,7 @@ def tile_advancedliquidneuralnetwork_pb_kernel(
             rstd = small.tile([P, 1], F32, tag="rstd")
             nc.gpsimd.tensor_scalar_add(out=rstd[:], in0=square_sum[:], scalar1=H * LN_EPS)
             nc.gpsimd.tensor_tensor(out=rstd[:], in0=rstd[:], in1=minus_half[:], op=ALU.pow)
-            nc.gpsimd.tensor_scalar(
+            engine.tensor_scalar(
                 out=u[:], in0=u[:], scalar1=minus_mean[:], scalar2=rstd[:],
                 op0=ALU.add, op1=ALU.mult,
             )
@@ -391,6 +391,8 @@ def tile_advancedliquidneuralnetwork_pb_kernel(
             nc.sync.dma_start(out=h_raw[q][:], in_=h_rows[q])
         add_bias_to_liq(4, nc.gpsimd)
         add_bias_to_liq(5, nc.gpsimd)
+        add_bias_to_liq(6, nc.gpsimd)
+        add_bias_to_liq(7, nc.gpsimd)
         win, finish_win = unit_k512(win_raw, win_mx)
         win(0, S)
         win(1, S)
@@ -402,8 +404,8 @@ def tile_advancedliquidneuralnetwork_pb_kernel(
         finish_win()
         add_att(0)
         add_att(1)
-        normalise(0)
-        normalise(1)
+        normalise(0, nc.gpsimd)
+        normalise(1, nc.gpsimd)
         xs(2, S)
         xs(3, S)
         compute_v(2)
@@ -411,8 +413,6 @@ def tile_advancedliquidneuralnetwork_pb_kernel(
         finish_xs()
         compute_v(3)
         quantise_v(1)
-        add_bias_to_liq(6, nc.gpsimd)
-        add_bias_to_liq(7, nc.gpsimd)
         spread(omr_cols, 0, omr_all)
         liq1, finish_liq1 = unit_k1024(liq_raw[1], liq_mx, 1)
         liq1(0, S)
@@ -422,11 +422,11 @@ def tile_advancedliquidneuralnetwork_pb_kernel(
         finish_liq1()
         compute_xin(0, range(0, 8))
         keep_h(0)
+        keep_h(1)
         add_att(2)
         add_att(3)
-        normalise(2)
-        normalise(3)
-        keep_h(1)
+        normalise(2, nc.gpsimd)
+        normalise(3, nc.gpsimd)
         compute_v(4)
         compute_v(5)
         quantise_v(2)
@@ -436,11 +436,10 @@ def tile_advancedliquidneuralnetwork_pb_kernel(
         tanh_times_r(0, range(4, 8), multiply_on_scalar)
         compute_xin(1, range(0, 4))
         keep_h(2)
-        keep_h(3)
         add_att(4)
         add_att(5)
-        normalise(4)
-        normalise(5)
+        normalise(4, nc.gpsimd)
+        normalise(5, nc.gpsimd)
         compute_v(6)
         compute_v(7)
         quantise_v(3)
@@ -448,15 +447,16 @@ def tile_advancedliquidneuralnetwork_pb_kernel(
         tanh_times_r(1, range(0, 4), multiply_on_scalar)
         add_xin(1, range(4, 8))
         tanh_times_r(1, range(4, 8), multiply_on_scalar)
+        keep_h(3)
         keep_h(4)
-        keep_h(5)
         finish(0, 0)
         finish(0, 1)
         compute_xin(1, range(4, 8))
         add_att(6)
         add_att(7)
-        normalise(6)
-        normalise(7)
+        normalise(6, nc.vector)
+        normalise(7, nc.vector)
+        keep_h(5)
         add_xin(2, range(0, 4))
         tanh_times_r(2, range(0, 4), multiply_on_scalar)
         add_xin(2, range(4, 8))

from contextlib import ExitStack

import concourse.mybir as mybir
from concourse.masks import make_identity

F32 = mybir.dt.float32
BF16 = mybir.dt.bfloat16
U32 = mybir.dt.uint32
U8 = mybir.dt.uint8
FP8X4 = mybir.dt.float8_e4m3fn_x4
ALU = mybir.AluOpType
ACT = mybir.ActivationFunctionType

P = 128
B, IN, H = 1024, 512, 1024
K_PASS = 512
BANK = 512
CHUNK = 512
TILES = CHUNK // P
GROUP = 2
GCOLS = GROUP * P
LN_EPS = 1e-5
TAU_EPS = 1e-6
SQRT_H = 32.0

FLOPS = 2 * B * H * (IN + H + H)


def tile_advancedliquidneuralnetwork_pb_kernel(
    tc, liq, h, x, W_in, b_in, W_v, b_v, W_o, b_o, g_att, beta_att, tau, out
):
    nc = tc.nc
    with ExitStack() as ctx:
        consts = ctx.enter_context(tc.tile_pool(name="consts", bufs=1))
        keep = ctx.enter_context(tc.tile_pool(name="keep", bufs=1))
        raw = ctx.enter_context(tc.tile_pool(name="raw", bufs=4))
        stage = ctx.enter_context(tc.tile_pool(name="stage", bufs=2))
        work = ctx.enter_context(tc.tile_pool(name="work", bufs=2))
        small = ctx.enter_context(tc.tile_pool(name="small", bufs=4))
        psum = ctx.enter_context(tc.psum_pool(name="psum", bufs=8))

        liq_rows = liq.rearrange("(q p i) k -> q p i k", q=2, i=TILES)
        h_rows = h.rearrange("(q p i) k -> q p i k", q=2, i=TILES)
        out_rows = out.rearrange("(q p i) n -> q p i n", q=2, i=TILES)
        wv_rows = W_v.rearrange("(g p t) k -> g p t k", g=2, t=4)
        wo_rows = W_o.rearrange("(q j p) k -> q p j k", q=2, p=P)

        vec_rows = consts.tile([P, P], BF16)
        nc.vector.memset(vec_rows[:], 0.0)
        ident = consts.tile([P, P], F32)
        make_identity(nc, ident[:])
        ident_bf = consts.tile([P, P], BF16)
        nc.vector.tensor_copy(out=ident_bf[:], in_=ident[:])
        minus_half = consts.tile([P, 1], F32)
        nc.vector.memset(minus_half[:], -0.5)

        liq_raw = [keep.tile([P, TILES, H], BF16, name="liq_raw%d" % q) for q in range(2)]
        for n, vector in enumerate((b_o, g_att, tau, beta_att, b_in)):
            nc.sync.dma_start(
                out=vec_rows[8 * n : 8 * n + 8, :], in_=vector.rearrange("(j p) -> j p", p=P)
            )
        bv = consts.tile([P, 8], BF16)
        nc.sync.dma_start(
            out=bv[:].rearrange("p (g t) -> p g t", t=4),
            in_=b_v.rearrange("(g p t) -> p g t", p=P, t=4),
        )

        warm = consts.tile([P, 2], F32)
        nc.vector.memset(warm[:], 0.0)
        nc.scalar.activation(out=warm[:, 1:2], in_=warm[:, 0:1], func=ACT.Tanh)

        vec_cols = consts.tile([P, 40], F32)
        r_cols = consts.tile([P, 8], F32)
        omr_cols = consts.tile([P, 8], F32)
        g_cols = consts.tile([P, 8], F32)
        xin_bias = consts.tile([P, 8], F32)
        bo_all = consts.tile([P, H], BF16)
        omr_all = consts.tile([P, H], F32)

        def make_vectors():
            bank = psum.tile([P, P], BF16, name="vec_bank", tag="bank")
            nc.tensor.transpose(bank[:], vec_rows[:], ident_bf[:])
            nc.vector.tensor_copy(out=vec_cols[:], in_=bank[:, 0:40])
            nc.vector.tensor_scalar_add(out=r_cols[:], in0=vec_cols[:, 16:24], scalar1=TAU_EPS)
            nc.vector.tensor_scalar_mul(out=g_cols[:], in0=vec_cols[:, 8:16], scalar1=SQRT_H)
            nc.vector.tensor_tensor(
                out=xin_bias[:], in0=vec_cols[:, 24:32], in1=vec_cols[:, 32:40], op=ALU.add
            )
            nc.vector.reciprocal(out=r_cols[:], in_=r_cols[:])
            nc.vector.tensor_scalar(
                out=omr_cols[:], in0=r_cols[:], scalar1=-1.0, scalar2=1.0,
                op0=ALU.mult, op1=ALU.add,
            )

        def spread(columns, first, result):
            for half in range(2):
                bank = psum.tile([P, 4, P], F32, name="spread", tag="bank")
                for j in range(4):
                    col = first + 4 * half + j
                    nc.tensor.transpose(
                        bank[:, j, :], columns[:, col : col + 1].to_broadcast([P, P]), ident[:]
                    )
                nc.scalar.copy(
                    out=result[:, half * BANK : (half + 1) * BANK],
                    in_=bank[:].rearrange("p j n -> p (j n)"),
                )

        def mx_operand(name, sets, passes, rows):
            codes = keep.tile([P, sets, passes, rows], U32, name=name + "_codes", align_bytes=64)
            scales = keep.tile([P, sets, passes, rows], U8, name=name + "_scales", align_bytes=64)
            return codes, scales

        liq_mx = mx_operand("liq", 2, 2, CHUNK)
        wv_mx = mx_operand("wv", 2, 2, CHUNK)
        v_mx = mx_operand("v", 4, 2, GCOLS)
        wo_mx = mx_operand("wo", 2, 2, CHUNK)
        x_mx = mx_operand("x", 2, 1, CHUNK)
        win_mx = mx_operand("win", 2, 1, CHUNK)

        def transpose_bank(word_blocks, grouped_words, copy):
            bank = psum.tile([P, 4, P], F32, tag="bank")
            for n, block in enumerate(word_blocks):
                nc.tensor.transpose(bank[:, n, :], block, ident[:])
            copy(out=grouped_words, in_=bank[:].rearrange("p (a u) r -> p a r u", u=2))

        def quantise(grouped, operand, s):
            codes, scales = operand
            nc.vector.quantize_mx(
                out=codes[:, s, :, :].rearrange("p c r -> p (c r)").bitcast(FP8X4),
                scales=scales[:, s, :, :].rearrange("p c r -> p (c r)"),
                in_=grouped.rearrange("p c r t -> p (c r t)"),
            )

        def unit_k1024(rows_raw, operand, chunk):
            words = rows_raw[:].bitcast(F32)
            grouped = stage.tile([P, 2, CHUNK, 4], BF16, tag="staged", align_bytes=64)
            grouped_words = grouped[:].bitcast(F32)

            def bank(i, copy):
                transpose_bank(
                    [words[:, i, 256 * a + u : 256 * (a + 1) : 2] for a in range(2) for u in range(2)],
                    grouped_words[:, :, i * P : (i + 1) * P, :],
                    copy,
                )

            def finish():
                quantise(grouped[:], operand, chunk)

            return bank, finish

        def unit_k512(rows_raw, operand):
            words = rows_raw[:].bitcast(F32)
            grouped = stage.tile([P, 2, CHUNK, 4], BF16, tag="staged", align_bytes=64)
            grouped_words = grouped[:].bitcast(F32)

            def bank(i, copy):
                transpose_bank(
                    [words[:, 2 * i + a, u:256:2] for a in range(2) for u in range(2)],
                    grouped_words[:, i // 2, GCOLS * (i % 2) : GCOLS * (i % 2 + 1), :].rearrange(
                        "p (a r) u -> p a r u", a=2
                    ),
                    copy,
                )

            def finish():
                for s in range(2):
                    quantise(grouped[:, s : s + 1, :, :], operand, s)

            return bank, finish

        def mx_matmul(acc, stationary, moving):
            (s_codes, s_scales), s_set, s_cols = stationary
            (m_codes, m_scales), m_set, m_cols = moving
            passes = s_codes.shape[2]
            for c in range(passes):
                nc.tensor.matmul_mx(
                    out=acc,
                    lhsT=s_codes[:, s_set, c, s_cols].bitcast(FP8X4),
                    lhsT_scale=s_scales[:, s_set, c, s_cols],
                    rhs=m_codes[:, m_set, c, m_cols].bitcast(FP8X4),
                    rhs_scale=m_scales[:, m_set, c, m_cols],
                    start=(c == 0),
                    stop=(c == passes - 1),
                )

        def tile_cols(n):
            return slice(n * P, (n + 1) * P)

        v_grouped = {}

        def compute_v(n):
            k, m = divmod(n, GROUP)
            if m == 0:
                v_grouped[k] = stage.tile(
                    [P, 2, GCOLS, 4], BF16, name="v_grouped", tag="v_grouped", bufs=2, align_bytes=64
                )
            for g in range(2):
                bank = psum.tile([P, 4, P], F32, tag="bank")
                for t in range(4):
                    mx_matmul(
                        bank[:, t, :], (wv_mx, g, tile_cols(t)),
                        (liq_mx, n // TILES, tile_cols(n % TILES)),
                    )
                nc.vector.tensor_tensor(
                    out=v_grouped[k][:, g, tile_cols(m), :],
                    in0=bank[:].rearrange("p t r -> p r t"),
                    in1=bv[:, 4 * g : 4 * g + 4].unsqueeze(1).to_broadcast([P, P, 4]),
                    op=ALU.add,
                )

        def quantise_v(k):
            quantise(v_grouped[k][:], v_mx, k)

        xin_t = keep.tile([P, 8, B], F32)

        def compute_xin(q, features):
            cols = slice(q * CHUNK, (q + 1) * CHUNK)
            for j in features:
                bank = psum.tile([P, BANK], F32, tag="bank")
                mx_matmul(
                    bank[:], (win_mx, j // TILES, tile_cols(j % TILES)), (x_mx, q, slice(0, CHUNK))
                )
                nc.scalar.activation(
                    out=xin_t[:, j, cols], in_=bank[:], func=ACT.Identity,
                    bias=xin_bias[:, j : j + 1], scale=1.0,
                )

        bank_cols = [slice(k * BANK, (k + 1) * BANK) for k in range(2)]
        residual, kept, tanh_of, sums_of = {}, {}, {}, {}

        def add_bias_to_liq(n, engine):
            q, i = divmod(n, TILES)
            residual[n] = work.tile([P, H], F32, name="residual", tag="residual", bufs=8)
            for cols in bank_cols if engine is nc.gpsimd else (slice(0, H),):
                engine.tensor_tensor(
                    out=residual[n][:, cols], in0=liq_raw[q][:, i, cols], in1=bo_all[:, cols],
                    op=ALU.add,
                )

        def keep_h(n):
            q, i = divmod(n, TILES)
            kept[n] = work.tile([P, H], F32, name="kept", tag="kept", bufs=6)
            for cols in bank_cols:
                nc.gpsimd.tensor_tensor(
                    out=kept[n][:, cols], in0=h_raw[q][:, i, cols], in1=omr_all[:, cols], op=ALU.mult
                )

        def add_att(n):
            u = residual[n]
            sums = small.tile([P, 2], F32, tag="sums")
            for k, cols in enumerate(bank_cols):
                att = psum.tile([P, BANK], F32, tag="bank")
                mx_matmul(
                    att[:], (v_mx, n // GROUP, tile_cols(n % GROUP)), (wo_mx, k, slice(0, CHUNK))
                )
                nc.vector.scalar_tensor_tensor(
                    out=u[:, cols], in0=att[:], scalar=1.0, in1=u[:, cols],
                    op0=ALU.mult, op1=ALU.add, accum_out=sums[:, k : k + 1],
                )
            sums_of[n] = sums

        def normalise(n, engine):
            u = residual[n]
            minus_mean = small.tile([P, 1], F32, tag="minus_mean")
            scaled_sums = small.tile([P, 2], F32, tag="scaled_sums")
            nc.scalar.activation(
                out=scaled_sums[:], in_=sums_of[n][:], func=ACT.Identity, scale=-1.0 / H,
                accum_out=minus_mean[:],
            )
            square_sum = small.tile([P, 1], F32, tag="square_sum")
            squares = work.tile([P, H], BF16, tag="squares", bufs=1)
            nc.scalar.activation(
                out=squares[:], in_=u[:], func=ACT.Square, bias=minus_mean[:], scale=1.0,
                accum_out=square_sum[:],
            )
            rstd = small.tile([P, 1], F32, tag="rstd")
            nc.gpsimd.tensor_scalar_add(out=rstd[:], in0=square_sum[:], scalar1=H * LN_EPS)
            nc.gpsimd.tensor_tensor(out=rstd[:], in0=rstd[:], in1=minus_half[:], op=ALU.pow)
            engine.tensor_scalar(
                out=u[:], in0=u[:], scalar1=minus_mean[:], scalar2=rstd[:],
                op0=ALU.add, op1=ALU.mult,
            )

        def add_xin(k, blocks):
            if k not in tanh_of:
                tanh_of[k] = work.tile([P, 8, GCOLS], F32, name="tanh", tag="tanh", bufs=2)
            t = tanh_of[k]
            cols = slice(k * GCOLS, (k + 1) * GCOLS)
            for first in blocks[::2]:
                bank = psum.tile([P, 2, GROUP, P], F32, tag="bank")
                for jj in range(2):
                    for m in range(GROUP):
                        nc.tensor.transpose(
                            bank[:, jj, m, :], residual[GROUP * k + m][:, tile_cols(first + jj)],
                            ident[:],
                        )
                for jj in range(2):
                    j = first + jj
                    nc.vector.scalar_tensor_tensor(
                        out=t[:, j, :], in0=bank[:, jj, :, :].rearrange("p m r -> p (m r)"),
                        scalar=g_cols[:, j : j + 1], in1=xin_t[:, j, cols],
                        op0=ALU.mult, op1=ALU.add,
                    )

        def tanh_times_r(k, blocks, multiply):
            t = tanh_of[k]
            part = t[:, blocks[0] : blocks[-1] + 1, :]
            nc.scalar.activation(out=part, in_=part, func=ACT.Tanh)
            for j in blocks:
                multiply(t[:, j, :], r_cols[:, j : j + 1])

        def multiply_on_scalar(values, factor):
            nc.scalar.mul(out=values, in_=values, mul=factor)

        def multiply_on_vector(values, factor):
            nc.vector.tensor_scalar_mul(out=values, in0=values, scalar1=factor)

        def finish(k, half):
            t = tanh_of[k]
            cols = bank_cols[half]
            for m in range(GROUP):
                n = GROUP * k + m
                q, i = divmod(n, TILES)
                bank = psum.tile([P, 4, P], F32, tag="bank")
                for j in range(4):
                    nc.tensor.transpose(bank[:, j, :], t[:, 4 * half + j, tile_cols(m)], ident[:])
                nc.vector.tensor_tensor(
                    out=kept[n][:, cols], in0=bank[:].rearrange("p j r -> p (j r)"),
                    in1=kept[n][:, cols], op=ALU.add,
                )
                nc.sync.dma_start(out=out_rows[q][:, i, cols], in_=kept[n][:, cols])

        ctx.enter_context(tc.manual_schedule(engines={mybir.EngineType.Pool}))
        V, S = nc.vector.tensor_copy, nc.scalar.copy

        for i in range(0, TILES, 2):
            nc.sync.dma_start(out=liq_raw[0][:, i : i + 2, :], in_=liq_rows[0][:, i : i + 2, :])
        wv_raw = [raw.tile([P, TILES, H], BF16, name="wv_raw%d" % g, tag="raw") for g in range(2)]
        for g in range(2):
            nc.sync.dma_start(out=wv_raw[g][:], in_=wv_rows[g])
        wo_raw = [raw.tile([P, TILES, H], BF16, name="wo_raw%d" % q, tag="raw") for q in range(2)]
        for q in range(2):
            nc.sync.dma_start(out=wo_raw[q][:], in_=wo_rows[q])
        liq0, finish_liq0 = unit_k1024(liq_raw[0], liq_mx, 0)
        liq0(0, V)
        liq0(1, S)
        liq0(2, V)
        liq0(3, S)
        make_vectors()
        spread(vec_cols, 0, bo_all)
        finish_liq0()
        wv0, finish_wv0 = unit_k1024(wv_raw[0], wv_mx, 0)
        wv0(0, V)
        wv0(1, S)
        wv0(2, V)
        wv0(3, S)
        add_bias_to_liq(0, nc.vector)
        add_bias_to_liq(1, nc.vector)
        finish_wv0()
        wv1, finish_wv1 = unit_k1024(wv_raw[1], wv_mx, 1)
        wv1(0, V)
        wv1(1, S)
        wv1(2, S)
        wv1(3, S)
        finish_wv1()
        nc.sync.dma_start(out=liq_raw[1][:], in_=liq_rows[1])
        win_raw = raw.tile([P, 8, IN], BF16, tag="raw")
        nc.sync.dma_start(out=win_raw[:], in_=W_in.rearrange("(j p) k -> p j k", p=P))
        x_raw = raw.tile([P, 8, IN], BF16, tag="raw")
        x_rows = x.rearrange("(q p i) k -> q p i k", q=2, i=TILES)
        for q in range(2):
            nc.sync.dma_start(out=x_raw[:, TILES * q : TILES * (q + 1), :], in_=x_rows[q])
        wo0, finish_wo0 = unit_k1024(wo_raw[0], wo_mx, 0)
        wo0(0, S)
        wo0(1, S)
        wo0(2, S)
        wo0(3, S)
        compute_v(0)
        add_bias_to_liq(2, nc.vector)
        finish_wo0()
        wo1, finish_wo1 = unit_k1024(wo_raw[1], wo_mx, 1)
        wo1(0, S)
        wo1(1, S)
        wo1(2, S)
        wo1(3, S)
        compute_v(1)
        finish_wo1()
        quantise_v(0)
        h_raw = [raw.tile([P, TILES, H], BF16, name="h_raw%d" % q, tag="raw") for q in range(2)]
        for q in range(2):
            nc.sync.dma_start(out=h_raw[q][:], in_=h_rows[q])
        add_bias_to_liq(4, nc.gpsimd)
        add_bias_to_liq(5, nc.gpsimd)
        add_bias_to_liq(6, nc.gpsimd)
        add_bias_to_liq(7, nc.gpsimd)
        win, finish_win = unit_k512(win_raw, win_mx)
        win(0, S)
        win(1, S)
        win(2, S)
        win(3, S)
        xs, finish_xs = unit_k512(x_raw, x_mx)
        xs(0, S)
        xs(1, S)
        finish_win()
        add_att(0)
        add_att(1)
        normalise(0, nc.gpsimd)
        normalise(1, nc.gpsimd)
        xs(2, S)
        xs(3, S)
        compute_v(2)
        add_bias_to_liq(3, nc.vector)
        finish_xs()
        compute_v(3)
        quantise_v(1)
        spread(omr_cols, 0, omr_all)
        liq1, finish_liq1 = unit_k1024(liq_raw[1], liq_mx, 1)
        liq1(0, S)
        liq1(1, S)
        liq1(2, S)
        liq1(3, S)
        finish_liq1()
        compute_xin(0, range(0, 8))
        keep_h(0)
        keep_h(1)
        add_att(2)
        add_att(3)
        normalise(2, nc.gpsimd)
        normalise(3, nc.gpsimd)
        compute_v(4)
        compute_v(5)
        quantise_v(2)
        add_xin(0, range(0, 4))
        tanh_times_r(0, range(0, 4), multiply_on_scalar)
        add_xin(0, range(4, 8))
        tanh_times_r(0, range(4, 8), multiply_on_scalar)
        compute_xin(1, range(0, 4))
        keep_h(2)
        add_att(4)
        add_att(5)
        normalise(4, nc.gpsimd)
        normalise(5, nc.gpsimd)
        compute_v(6)
        compute_v(7)
        quantise_v(3)
        add_xin(1, range(0, 4))
        tanh_times_r(1, range(0, 4), multiply_on_scalar)
        add_xin(1, range(4, 8))
        tanh_times_r(1, range(4, 8), multiply_on_scalar)
        keep_h(3)
        keep_h(4)
        finish(0, 0)
        finish(0, 1)
        compute_xin(1, range(4, 8))
        add_att(6)
        add_att(7)
        normalise(6, nc.vector)
        normalise(7, nc.vector)
        keep_h(5)
        add_xin(2, range(0, 4))
        tanh_times_r(2, range(0, 4), multiply_on_scalar)
        add_xin(2, range(4, 8))
        tanh_times_r(2, range(4, 8), multiply_on_scalar)
        finish(1, 0)
        finish(1, 1)
        keep_h(6)
        keep_h(7)
        add_xin(3, range(0, 2))
        tanh_times_r(3, range(0, 2), multiply_on_scalar)
        add_xin(3, range(2, 4))
        tanh_times_r(3, range(2, 4), multiply_on_vector)
        finish(2, 0)
        add_xin(3, range(4, 6))
        tanh_times_r(3, range(4, 6), multiply_on_scalar)
        add_xin(3, range(6, 8))
        tanh_times_r(3, range(6, 8), multiply_on_vector)
        finish(2, 1)
        finish(3, 0)
        finish(3, 1)
